import numpy as np
import ml_dtypes


def mxq(x, axis, fmt="e4m3"):
    dtype, down = {"e4m3": (ml_dtypes.float8_e4m3fn, 7), "e5m2": (ml_dtypes.float8_e5m2, 14)}[fmt]
    v = np.moveaxis(np.asarray(x, np.float32).astype(ml_dtypes.bfloat16).astype(np.float64), axis, -1)
    blocks = v.reshape(v.shape[:-1] + (-1, 32))
    amax = np.abs(blocks).max(-1, keepdims=True)
    byte = np.maximum(np.where(amax > 0, np.frexp(amax)[1] - 1 + 127, 0) - down, 1)
    scale = np.exp2(byte - 127.0)
    codes = (blocks / scale).astype(np.float32).astype(dtype).astype(np.float64)
    return np.moveaxis((codes * scale).reshape(v.shape), -1, axis)


WIDE = False


def mx_kscale(k):
    if not WIDE:
        return np.ones(k)
    levels = np.array([10, -10, 5, -5, 0])
    if k % 512:
        return np.exp2(np.random.permutation(np.resize(levels, k // 32))).repeat(32)
    a = np.empty((k // 512, 16))
    for p in range(k // 512):
        a[p, :8] = np.random.permutation(np.resize(levels, 8))
        for g in range(8):
            far = levels[np.abs(levels - a[p, g]) >= 10]
            a[p, g + 8] = far[np.random.randint(len(far))]
    return np.exp2(a.ravel()).repeat(32)


BF16 = ml_dtypes.bfloat16


def bf(x):
    return np.asarray(x, np.float32).astype(BF16)


def f64(x):
    return np.asarray(x).astype(np.float64)


B, Q, K, D = 4, 256, 256, 512
SIG = 2.0
PMASK = 0.1


def setup_inputs():
    s = mx_kscale(D)
    q = np.random.standard_normal((B, Q, D)) * s
    k = np.random.standard_normal((B, K, D)) * (SIG / np.sqrt(D)) / s
    k[:, :, 0] = np.where(np.random.random((B, K)) < PMASK, 0.0, k[:, :, 0])
    temperature = 1.0 + 0.1 * np.random.standard_normal(1)
    bias = -(np.log(K) + SIG ** 2 / 2.0) + 0.1 * np.random.standard_normal(1)
    return {"queries": bf(q), "keys": bf(k), "temperature": bf(temperature), "bias": bf(bias)}


def reference(queries, keys, temperature, bias):
    kf = f64(keys)
    logits = mxq(f64(queries), 2, "e4m3") @ mxq(kf, 2, "e4m3").transpose(0, 2, 1)
    key_mask = (kf[:, :, 0] == 0.0)[:, None, :]
    logits = np.where(key_mask, -np.inf, logits)
    m = logits.max(-1, keepdims=True)
    e = np.exp(logits - m)
    z = e.sum(-1, keepdims=True)
    approx_max_logit = (np.log(z) + m)[:, :, 0]
    confidence = 1.0 / (1.0 + np.exp(-((approx_max_logit + f64(bias)) * f64(temperature))))
    attn = e / z
    return attn, confidence

@@ -1,0 +1,229 @@
+from contextlib import ExitStack
+
+import concourse.mybir as mybir
+from concourse.masks import make_identity
+
+F32 = mybir.dt.float32
+BF16 = mybir.dt.bfloat16
+U32 = mybir.dt.uint32
+U8 = mybir.dt.uint8
+FP8X4 = mybir.dt.float8_e4m3fn_x4
+ALU = mybir.AluOpType
+ACT = mybir.ActivationFunctionType
+AXIS = mybir.AxisListType
+
+B, Q, K, D = 4, 256, 256, 512
+P = 128
+ROW_TILES = Q // P
+PACK = 4
+WORDS = D // 2
+HALVES = WORDS // P
+BANK = 512
+STATS = B * ROW_TILES
+AHEAD = 2
+MASKED = -(2.0**100)
+
+FLOPS = 2 * B * Q * K * D
+
+
+def tile_contentattention_s_kernel(tc, queries, keys, temperature, bias, out_0, out_1):
+    nc = tc.nc
+    with ExitStack() as ctx:
+        ctx.enter_context(tc.manual_schedule())
+        consts = ctx.enter_context(tc.tile_pool(name="consts", bufs=1))
+        per_batch = ctx.enter_context(tc.tile_pool(name="per_batch", bufs=B))
+        psum = ctx.enter_context(tc.psum_pool(name="psum", bufs=2))
+
+        temp_bf = consts.tile([P, 1], BF16)
+        nc.scalar.dma_start(out=temp_bf[:], in_=temperature.partition_broadcast(P))
+        bias_bf = consts.tile([P, 1], BF16)
+        nc.scalar.dma_start(out=bias_bf[:], in_=bias.partition_broadcast(P))
+
+        k_rows = []
+        q_rows = []
+        for b in range(B):
+            k_sb = per_batch.tile([P, ROW_TILES * D], BF16)
+            q_sb = per_batch.tile([P, ROW_TILES * D], BF16)
+            k_tiles = keys[b].rearrange("(p n) d -> p n d", n=ROW_TILES)
+            q_tiles = queries[b].rearrange("(n p) d -> p n d", p=P)
+            for n in range(ROW_TILES):
+                nc.sync.dma_start(out=k_sb[:, n * D : (n + 1) * D], in_=k_tiles[:, n, :])
+            for n in range(ROW_TILES):
+                nc.sync.dma_start(out=q_sb[:, n * D : (n + 1) * D], in_=q_tiles[:, n, :])
+            k_rows.append(k_sb)
+            q_rows.append(q_sb)
+
+        ident = consts.tile([P, P], F32)
+        nc.vector.memset(ident[:], 0.0)
+        make_identity(nc, ident[:], nomemset=True)
+        conf_cols = consts.tile([P, P], F32)
+        nc.vector.memset(conf_cols[:], 0.0)
+        scratch = consts.tile([P, 1], F32)
+        nc.vector.memset(scratch[:], 0.0)
+        nc.scalar.activation(out=scratch[:], in_=scratch[:], func=ACT.Exp)
+
+        temp = consts.tile([P, 1], F32)
+        nc.vector.tensor_copy(out=temp[:], in_=temp_bf[:])
+        neg_temp = consts.tile([P, 1], F32)
+        nc.vector.tensor_scalar_mul(out=neg_temp[:], in0=temp_bf[:], scalar1=-1.0)
+        neg_bias_temp = consts.tile([P, 1], F32)
+        nc.vector.scalar_tensor_tensor(
+            out=neg_bias_temp[:], in0=bias_bf[:], scalar=-1.0, in1=temp_bf[:], op0=ALU.mult, op1=ALU.mult
+        )
+
+        neg_max = consts.tile([P, STATS], F32)
+        row_sum = consts.tile([P, STATS], F32)
+        inv_sum = consts.tile([P, STATS], F32)
+        sum_pow = consts.tile([P, STATS], F32)
+        exp_part = consts.tile([P, STATS], F32)
+
+        penalty_cols = []
+        for b in range(B):
+            penalty_col = per_batch.tile([P, ROW_TILES], BF16)
+            nc.gpsimd.tensor_scalar(
+                out=penalty_col[:].rearrange("p (n o) -> p n o", o=1),
+                in0=k_rows[b][:].rearrange("p (n d) -> p n d", n=ROW_TILES)[:, :, 0:1],
+                scalar1=0.0,
+                scalar2=MASKED,
+                op0=ALU.is_equal,
+                op1=ALU.mult,
+            )
+            penalty_cols.append(penalty_col)
+
+        def transpose_words(rows, bank):
+            words = rows[:].bitcast(F32)
+            for n in range(ROW_TILES):
+                for h in range(HALVES):
+                    piece = n * HALVES + h
+                    nc.tensor.transpose(
+                        out=bank[:, piece * P : (piece + 1) * P],
+                        in_=words[:, n * WORDS + h : (n + 1) * WORDS : HALVES],
+                        identity=ident[:],
+                    )
+
+        operands = {}
+        exps = {}
+
+        def prepare(b, copy_keys):
+            k_bank = psum.tile([P, BANK], F32)
+            transpose_words(k_rows[b], k_bank)
+            q_bank = psum.tile([P, BANK], F32)
+            transpose_words(q_rows[b], q_bank)
+            penalty_bank = psum.tile([P, BANK], F32)
+            nc.tensor.transpose(
+                out=penalty_bank[:, 0:P],
+                in_=penalty_cols[b][:].bitcast(F32).to_broadcast([P, P]),
+                identity=ident[:],
+            )
+
+            k_grouped = per_batch.tile([P, K * PACK], BF16, align_bytes=64)
+            copy_keys(
+                out=k_grouped[:].bitcast(F32).rearrange("w (p n h) -> w p n h", n=ROW_TILES, h=HALVES),
+                in_=k_bank[:].rearrange("w (n h p) -> w p n h", n=ROW_TILES, h=HALVES),
+            )
+            q_grouped = per_batch.tile([P, Q * PACK], BF16, align_bytes=64)
+            nc.scalar.copy(
+                out=q_grouped[:].bitcast(F32).rearrange("w (n p h) -> w n p h", n=ROW_TILES, h=HALVES),
+                in_=q_bank[:].rearrange("w (n h p) -> w n p h", n=ROW_TILES, h=HALVES),
+            )
+            penalty = per_batch.tile([P, K], BF16)
+            nc.scalar.copy(out=penalty[:].bitcast(F32), in_=penalty_bank[:, 0:P])
+
+            k_codes = per_batch.tile([P, K], U32, align_bytes=64)
+            k_scales = per_batch.tile([P, K], U8, align_bytes=64)
+            nc.vector.quantize_mx(out=k_codes[:].bitcast(FP8X4), scales=k_scales[:], in_=k_grouped[:])
+            q_codes = per_batch.tile([P, Q], U32, align_bytes=64)
+            q_scales = per_batch.tile([P, Q], U8, align_bytes=64)
+            nc.vector.quantize_mx(out=q_codes[:].bitcast(FP8X4), scales=q_scales[:], in_=q_grouped[:])
+            operands[b] = (k_codes, k_scales, q_codes, q_scales, penalty)
+
+        def masked_logits(b):
+            k_codes, k_scales, q_codes, q_scales, penalty = operands[b]
+            logits = psum.tile([P, ROW_TILES * K], F32)
+            for n in range(ROW_TILES):
+                q_cols = slice(n * P, (n + 1) * P)
+                nc.tensor.matmul_mx(
+                    out=logits[:, n * K : (n + 1) * K],
+                    lhsT=q_codes[:, q_cols].bitcast(FP8X4),
+                    lhsT_scale=q_scales[:, q_cols],
+                    rhs=k_codes[:].bitcast(FP8X4),
+                    rhs_scale=k_scales[:],
+                    start=True,
+                    stop=True,
+                )
+            masked = per_batch.tile([P, ROW_TILES, K], F32)
+            nc.vector.tensor_tensor(
+                out=masked[:],
+                in0=logits[:].rearrange("p (n k) -> p n k", n=ROW_TILES),
+                in1=penalty[:].unsqueeze(1).to_broadcast([P, ROW_TILES, K]),
+                op=ALU.add,
+            )
+            for n in range(ROW_TILES):
+                col = b * ROW_TILES + n
+                nc.vector.tensor_reduce(
+                    out=neg_max[:, col : col + 1], in_=masked[:, n, :], axis=AXIS.X, op=ALU.max, negate=True
+                )
+            return masked
+
+        def exponentials(b, masked):
+            expd = per_batch.tile([P, ROW_TILES, K], F32)
+            for n in range(ROW_TILES):
+                col = b * ROW_TILES + n
+                nc.scalar.activation(
+                    out=expd[:, n, :],
+                    in_=masked[:, n, :],
+                    func=ACT.Exp,
+                    bias=neg_max[:, col : col + 1],
+                    accum_out=row_sum[:, col : col + 1],
+                )
+            stat_cols = slice(b * ROW_TILES, (b + 1) * ROW_TILES)
+            nc.gpsimd.tensor_tensor(
+                out=sum_pow[:, stat_cols],
+                in0=row_sum[:, stat_cols],
+                in1=neg_temp[:].to_broadcast([P, ROW_TILES]),
+                op=ALU.pow,
+            )
+            nc.scalar.activation(
+                out=exp_part[:, stat_cols],
+                in_=neg_max[:, stat_cols],
+                func=ACT.Exp,
+                scale=temp[:],
+                bias=neg_bias_temp[:],
+            )
+            exps[b] = expd
+
+        def normalise(b):
+            expd = exps[b]
+            first = b * ROW_TILES
+            stat_cols = slice(first, first + ROW_TILES)
+            nc.vector.reciprocal(out=inv_sum[:, stat_cols], in_=row_sum[:, stat_cols])
+            attn = per_batch.tile([P, ROW_TILES, K], F32)
+            for n in range(ROW_TILES):
+                nc.scalar.activation(
+                    out=attn[:, n, :],
+                    in_=expd[:, n, :],
+                    func=ACT.Copy,
+                    scale=inv_sum[:, first + n : first + n + 1],
+                )
+                nc.sync.dma_start(out=out_0[b, n * P : (n + 1) * P, :], in_=attn[:, n, :])
+
+        for b in range(AHEAD):
+            prepare(b, nc.vector.tensor_copy)
+        for b in range(B):
+            masked = masked_logits(b)
+            if b + AHEAD < B:
+                prepare(b + AHEAD, nc.scalar.copy)
+            exponentials(b, masked)
+            if b >= 1:
+                normalise(b - 1)
+        normalise(B - 1)
+
+        denom = consts.tile([P, STATS], F32)
+        nc.vector.tensor_tensor(out=denom[:], in0=sum_pow[:], in1=exp_part[:], op=ALU.mult)
+        nc.vector.tensor_scalar_add(out=denom[:], in0=denom[:], scalar1=1.0)
+        nc.vector.reciprocal(out=conf_cols[:, 0:STATS], in_=denom[:])
+        conf_bank = psum.tile([P, BANK], F32, tag="penalty_bank")
+        nc.tensor.transpose(out=conf_bank[:, 0:P], in_=conf_cols[:], identity=ident[:])
+        conf_rows = consts.tile([P, P], F32)
+        nc.vector.tensor_copy(out=conf_rows[:], in_=conf_bank[:, 0:P])
+        nc.sync.dma_start(out=out_1.rearrange("b (n p) -> (b n) p", p=P), in_=conf_rows[0:STATS, :])

@@ -20,7 +20,6 @@ WORDS = D // 2
 HALVES = WORDS // P
 BANK = 512
 STATS = B * ROW_TILES
-AHEAD = 2
 MASKED = -(2.0**100)
 
 FLOPS = 2 * B * Q * K * D
@@ -32,7 +31,7 @@ def tile_contentattention_s_kernel(tc, queries, keys, temperature, bias, out_0, 
         ctx.enter_context(tc.manual_schedule())
         consts = ctx.enter_context(tc.tile_pool(name="consts", bufs=1))
         per_batch = ctx.enter_context(tc.tile_pool(name="per_batch", bufs=B))
-        psum = ctx.enter_context(tc.psum_pool(name="psum", bufs=2))
+        psum = ctx.enter_context(tc.psum_pool(name="psum", bufs=8))
 
         temp_bf = consts.tile([P, 1], BF16)
         nc.scalar.dma_start(out=temp_bf[:], in_=temperature.partition_broadcast(P))
@@ -44,20 +43,21 @@ def tile_contentattention_s_kernel(tc, queries, keys, temperature, bias, out_0, 
         for b in range(B):
             k_sb = per_batch.tile([P, ROW_TILES * D], BF16)
             q_sb = per_batch.tile([P, ROW_TILES * D], BF16)
-            k_tiles = keys[b].rearrange("(p n) d -> p n d", n=ROW_TILES)
+            k_tiles = keys[b].rearrange("(n p) d -> p n d", p=P)
             q_tiles = queries[b].rearrange("(n p) d -> p n d", p=P)
-            for n in range(ROW_TILES):
-                nc.sync.dma_start(out=k_sb[:, n * D : (n + 1) * D], in_=k_tiles[:, n, :])
-            for n in range(ROW_TILES):
-                nc.sync.dma_start(out=q_sb[:, n * D : (n + 1) * D], in_=q_tiles[:, n, :])
             k_rows.append(k_sb)
             q_rows.append(q_sb)
+            for sb, dram in ((k_sb, k_tiles), (q_sb, q_tiles)):
+                for n in range(ROW_TILES):
+                    nc.sync.dma_start(out=sb[:, n * D : (n + 1) * D], in_=dram[:, n, :])
 
         ident = consts.tile([P, P], F32)
         nc.vector.memset(ident[:], 0.0)
         make_identity(nc, ident[:], nomemset=True)
         conf_cols = consts.tile([P, P], F32)
         nc.vector.memset(conf_cols[:], 0.0)
+        ones = consts.tile([P, 1], F32)
+        nc.vector.memset(ones[:], 1.0)
         scratch = consts.tile([P, 1], F32)
         nc.vector.memset(scratch[:], 0.0)
         nc.scalar.activation(out=scratch[:], in_=scratch[:], func=ACT.Exp)
@@ -76,6 +76,7 @@ def tile_contentattention_s_kernel(tc, queries, keys, temperature, bias, out_0, 
         inv_sum = consts.tile([P, STATS], F32)
         sum_pow = consts.tile([P, STATS], F32)
         exp_part = consts.tile([P, STATS], F32)
+        denom = consts.tile([P, STATS], F32)
 
         penalty_cols = []
         for b in range(B):
@@ -90,56 +91,64 @@ def tile_contentattention_s_kernel(tc, queries, keys, temperature, bias, out_0, 
             )
             penalty_cols.append(penalty_col)
 
-        def transpose_words(rows, bank):
-            words = rows[:].bitcast(F32)
-            for n in range(ROW_TILES):
+        def words_of(rows, n, h):
+            return rows[:].bitcast(F32)[:, n * WORDS + h : (n + 1) * WORDS : HALVES]
+
+        def transpose_tiles(rows, tiles):
+            bank = psum.tile([P, BANK], F32, name="bank")
+            for i, n in enumerate(tiles):
                 for h in range(HALVES):
-                    piece = n * HALVES + h
+                    piece = i * HALVES + h
                     nc.tensor.transpose(
-                        out=bank[:, piece * P : (piece + 1) * P],
-                        in_=words[:, n * WORDS + h : (n + 1) * WORDS : HALVES],
-                        identity=ident[:],
+                        out=bank[:, piece * P : (piece + 1) * P], in_=words_of(rows, n, h), identity=ident[:]
                     )
+            return bank
 
-        operands = {}
-        exps = {}
-
-        def prepare(b, copy_keys):
-            k_bank = psum.tile([P, BANK], F32)
-            transpose_words(k_rows[b], k_bank)
-            q_bank = psum.tile([P, BANK], F32)
-            transpose_words(q_rows[b], q_bank)
-            penalty_bank = psum.tile([P, BANK], F32)
+        def transpose_penalty(b):
+            bank = psum.tile([P, BANK], F32, name="bank")
             nc.tensor.transpose(
-                out=penalty_bank[:, 0:P],
-                in_=penalty_cols[b][:].bitcast(F32).to_broadcast([P, P]),
-                identity=ident[:],
+                out=bank[:, 0:P], in_=penalty_cols[b][:].bitcast(F32).to_broadcast([P, P]), identity=ident[:]
+            )
+            return bank
+
+        def group_tile(name):
+            return per_batch.tile([P, K * PACK], BF16, align_bytes=64, name=name)
+
+        k_grouped = [group_tile("k_grouped") for b in range(B)]
+        q_grouped = [group_tile("q_grouped") for b in range(B)]
+
+        def copy_words(copy, grouped, bank, tiles):
+            first, count = tiles[0], len(tiles)
+            copy(
+                out=grouped[:, first * P * PACK : (first + count) * P * PACK]
+                .bitcast(F32)
+                .rearrange("w (n p h) -> w n p h", n=count, h=HALVES),
+                in_=bank[:, 0 : count * HALVES * P].rearrange("w (n h p) -> w n p h", n=count, h=HALVES),
             )
 
-            k_grouped = per_batch.tile([P, K * PACK], BF16, align_bytes=64)
-            copy_keys(
-                out=k_grouped[:].bitcast(F32).rearrange("w (p n h) -> w p n h", n=ROW_TILES, h=HALVES),
-                in_=k_bank[:].rearrange("w (n h p) -> w p n h", n=ROW_TILES, h=HALVES),
-            )
-            q_grouped = per_batch.tile([P, Q * PACK], BF16, align_bytes=64)
-            nc.scalar.copy(
-                out=q_grouped[:].bitcast(F32).rearrange("w (n p h) -> w n p h", n=ROW_TILES, h=HALVES),
-                in_=q_bank[:].rearrange("w (n h p) -> w n p h", n=ROW_TILES, h=HALVES),
-            )
+        penalties = {}
+
+        def copy_penalty(copy, b, bank):
             penalty = per_batch.tile([P, K], BF16)
-            nc.scalar.copy(out=penalty[:].bitcast(F32), in_=penalty_bank[:, 0:P])
+            copy(out=penalty[:].bitcast(F32), in_=bank[:, 0:P])
+            penalties[b] = penalty
 
+        codes = {}
+
+        def quantize(b):
             k_codes = per_batch.tile([P, K], U32, align_bytes=64)
             k_scales = per_batch.tile([P, K], U8, align_bytes=64)
-            nc.vector.quantize_mx(out=k_codes[:].bitcast(FP8X4), scales=k_scales[:], in_=k_grouped[:])
+            nc.vector.quantize_mx(out=k_codes[:].bitcast(FP8X4), scales=k_scales[:], in_=k_grouped[b][:])
             q_codes = per_batch.tile([P, Q], U32, align_bytes=64)
             q_scales = per_batch.tile([P, Q], U8, align_bytes=64)
-            nc.vector.quantize_mx(out=q_codes[:].bitcast(FP8X4), scales=q_scales[:], in_=q_grouped[:])
-            operands[b] = (k_codes, k_scales, q_codes, q_scales, penalty)
+            nc.vector.quantize_mx(out=q_codes[:].bitcast(FP8X4), scales=q_scales[:], in_=q_grouped[b][:])
+            codes[b] = (k_codes, k_scales, q_codes, q_scales)
 
-        def masked_logits(b):
-            k_codes, k_scales, q_codes, q_scales, penalty = operands[b]
-            logits = psum.tile([P, ROW_TILES * K], F32)
+        logits_banks = {}
+
+        def multiply(b):
+            k_codes, k_scales, q_codes, q_scales = codes[b]
+            logits = psum.tile([P, BANK], F32, name="bank")
             for n in range(ROW_TILES):
                 q_cols = slice(n * P, (n + 1) * P)
                 nc.tensor.matmul_mx(
@@ -151,79 +160,139 @@ def tile_contentattention_s_kernel(tc, queries, keys, temperature, bias, out_0, 
                     start=True,
                     stop=True,
                 )
+            logits_banks[b] = logits
+
+        masked_tiles = {}
+
+        def add_mask(b):
             masked = per_batch.tile([P, ROW_TILES, K], F32)
             nc.vector.tensor_tensor(
-                out=masked[:],
-                in0=logits[:].rearrange("p (n k) -> p n k", n=ROW_TILES),
-                in1=penalty[:].unsqueeze(1).to_broadcast([P, ROW_TILES, K]),
+                out=masked[:].rearrange("p n (m k) -> p n m k", k=P),
+                in0=logits_banks[b][:].rearrange("p (n m k) -> p n m k", n=ROW_TILES, k=P),
+                in1=penalties[b][:]
+                .rearrange("p (k m) -> p m k", m=ROW_TILES)
+                .unsqueeze(1)
+                .to_broadcast([P, ROW_TILES, ROW_TILES, P]),
                 op=ALU.add,
             )
-            for n in range(ROW_TILES):
-                col = b * ROW_TILES + n
-                nc.vector.tensor_reduce(
-                    out=neg_max[:, col : col + 1], in_=masked[:, n, :], axis=AXIS.X, op=ALU.max, negate=True
-                )
-            return masked
+            masked_tiles[b] = masked
 
-        def exponentials(b, masked):
+        def maxima(first, last):
+            b, n = divmod(first, ROW_TILES)
+            nc.vector.tensor_reduce(
+                out=neg_max[:, first:last],
+                in_=masked_tiles[b][:, n : n + last - first, :],
+                axis=AXIS.X,
+                op=ALU.max,
+                negate=True,
+            )
+
+        exps = {}
+
+        def exponentials(b):
             expd = per_batch.tile([P, ROW_TILES, K], F32)
             for n in range(ROW_TILES):
                 col = b * ROW_TILES + n
                 nc.scalar.activation(
                     out=expd[:, n, :],
-                    in_=masked[:, n, :],
+                    in_=masked_tiles[b][:, n, :],
                     func=ACT.Exp,
                     bias=neg_max[:, col : col + 1],
                     accum_out=row_sum[:, col : col + 1],
                 )
-            stat_cols = slice(b * ROW_TILES, (b + 1) * ROW_TILES)
-            nc.gpsimd.tensor_tensor(
-                out=sum_pow[:, stat_cols],
-                in0=row_sum[:, stat_cols],
-                in1=neg_temp[:].to_broadcast([P, ROW_TILES]),
-                op=ALU.pow,
-            )
-            nc.scalar.activation(
-                out=exp_part[:, stat_cols],
-                in_=neg_max[:, stat_cols],
-                func=ACT.Exp,
-                scale=temp[:],
-                bias=neg_bias_temp[:],
-            )
             exps[b] = expd
 
-        def normalise(b):
-            expd = exps[b]
-            first = b * ROW_TILES
-            stat_cols = slice(first, first + ROW_TILES)
-            nc.vector.reciprocal(out=inv_sum[:, stat_cols], in_=row_sum[:, stat_cols])
-            attn = per_batch.tile([P, ROW_TILES, K], F32)
-            for n in range(ROW_TILES):
+        def powers(first, last):
+            cols = slice(first, last)
+            nc.gpsimd.tensor_tensor(
+                out=sum_pow[:, cols],
+                in0=row_sum[:, cols],
+                in1=neg_temp[:].to_broadcast([P, last - first]),
+                op=ALU.pow,
+            )
+
+        def exponential_parts():
+            nc.scalar.activation(
+                out=exp_part[:], in_=neg_max[:], func=ACT.Exp, scale=temp[:], bias=neg_bias_temp[:]
+            )
+
+        attn = consts.tile([P, STATS, K], F32)
+
+        def invert(first, last):
+            cols = slice(first * ROW_TILES, last * ROW_TILES)
+            nc.vector.reciprocal(out=inv_sum[:, cols], in_=row_sum[:, cols])
+
+        def normalise(b, n, on_scalar):
+            col = b * ROW_TILES + n
+            if on_scalar:
                 nc.scalar.activation(
-                    out=attn[:, n, :],
-                    in_=expd[:, n, :],
-                    func=ACT.Copy,
-                    scale=inv_sum[:, first + n : first + n + 1],
+                    out=attn[:, col, :], in_=exps[b][:, n, :], func=ACT.Copy, scale=inv_sum[:, col : col + 1]
                 )
-                nc.sync.dma_start(out=out_0[b, n * P : (n + 1) * P, :], in_=attn[:, n, :])
+            else:
+                nc.vector.tensor_scalar_mul(
+                    out=attn[:, col, :], in0=exps[b][:, n, :], scalar1=inv_sum[:, col : col + 1]
+                )
+            nc.sync.dma_start(out=out_0[b, n * P : (n + 1) * P, :], in_=attn[:, col, :])
 
-        for b in range(AHEAD):
-            prepare(b, nc.vector.tensor_copy)
+        def denominators(b):
+            for col in range(b * ROW_TILES, (b + 1) * ROW_TILES):
+                nc.vector.scalar_tensor_tensor(
+                    out=denom[:, col : col + 1],
+                    in0=sum_pow[:, col : col + 1],
+                    scalar=exp_part[:, col : col + 1],
+                    in1=ones[:],
+                    op0=ALU.mult,
+                    op1=ALU.add,
+                )
+
+        vcopy, scopy = nc.vector.tensor_copy, nc.scalar.copy
+
+        def prepare(b, k_copy):
+            copy_words(k_copy, k_grouped[b], transpose_tiles(k_rows[b], [0, 1]), [0, 1])
+            copy_words(scopy, q_grouped[b], transpose_tiles(q_rows[b], [0, 1]), [0, 1])
+            copy_penalty(scopy, b, transpose_penalty(b))
+
+        for n in range(ROW_TILES):
+            copy_words(vcopy, k_grouped[0], transpose_tiles(k_rows[0], [n]), [n])
+        for n in range(ROW_TILES):
+            copy_words(scopy, q_grouped[0], transpose_tiles(q_rows[0], [n]), [n])
+        copy_penalty(scopy, 0, transpose_penalty(0))
+        quantize(0)
+        prepare(1, vcopy)
+        multiply(0)
         for b in range(B):
-            masked = masked_logits(b)
-            if b + AHEAD < B:
-                prepare(b + AHEAD, nc.scalar.copy)
-            exponentials(b, masked)
-            if b >= 1:
-                normalise(b - 1)
-        normalise(B - 1)
+            if b + 2 < B:
+                prepare(b + 2, scopy)
+            add_mask(b)
+            if b + 1 < B:
+                quantize(b + 1)
+                multiply(b + 1)
+                maxima(2 * b, 2 * b + 2)
+            else:
+                maxima(2 * b, 2 * b + 1)
+                maxima(2 * b + 1, 2 * b + 2)
+            exponentials(b)
+            if b + 1 < B:
+                powers(2 * b, 2 * b + 2)
+            if 1 <= b < B - 1:
+                invert(b - 1, b)
+                normalise(b - 1, 0, True)
+                normalise(b - 1, 1, True)
+        powers(STATS - 2, STATS - 1)
+        powers(STATS - 1, STATS)
+        exponential_parts()
+        invert(B - 2, B - 1)
+        normalise(B - 2, 0, False)
+        normalise(B - 2, 1, False)
+        invert(B - 1, B)
+        normalise(B - 1, 0, True)
+        normalise(B - 1, 1, False)
+        for b in range(B):
+            denominators(b)
 
-        denom = consts.tile([P, STATS], F32)
-        nc.vector.tensor_tensor(out=denom[:], in0=sum_pow[:], in1=exp_part[:], op=ALU.mult)
-        nc.vector.tensor_scalar_add(out=denom[:], in0=denom[:], scalar1=1.0)
         nc.vector.reciprocal(out=conf_cols[:, 0:STATS], in_=denom[:])
-        conf_bank = psum.tile([P, BANK], F32, tag="penalty_bank")
+        conf_bank = psum.tile([P, BANK], F32, name="bank")
         nc.tensor.transpose(out=conf_bank[:, 0:P], in_=conf_cols[:], identity=ident[:])
-        conf_rows = consts.tile([P, P], F32)
-        nc.vector.tensor_copy(out=conf_rows[:], in_=conf_bank[:, 0:P])
-        nc.sync.dma_start(out=out_1.rearrange("b (n p) -> (b n) p", p=P), in_=conf_rows[0:STATS, :])
+        conf_rows = consts.tile([STATS, P], F32)
+        nc.vector.tensor_copy(out=conf_rows[:], in_=conf_bank[0:STATS, 0:P])
+        nc.sync.dma_start(out=out_1.rearrange("b (n p) -> (b n) p", p=P), in_=conf_rows[:])

@@ -166,15 +166,13 @@ def tile_contentattention_s_kernel(tc, queries, keys, temperature, bias, out_0, 
 
         def add_mask(b):
             masked = per_batch.tile([P, ROW_TILES, K], F32)
-            nc.vector.tensor_tensor(
-                out=masked[:].rearrange("p n (m k) -> p n m k", k=P),
-                in0=logits_banks[b][:].rearrange("p (n m k) -> p n m k", n=ROW_TILES, k=P),
-                in1=penalties[b][:]
-                .rearrange("p (k m) -> p m k", m=ROW_TILES)
-                .unsqueeze(1)
-                .to_broadcast([P, ROW_TILES, ROW_TILES, P]),
-                op=ALU.add,
-            )
+            for n in range(ROW_TILES):
+                nc.vector.tensor_tensor(
+                    out=masked[:, n, :].rearrange("p (m k) -> p m k", k=P),
+                    in0=logits_banks[b][:, n * K : (n + 1) * K].rearrange("p (m k) -> p m k", k=P),
+                    in1=penalties[b][:].rearrange("p (k m) -> p m k", m=ROW_TILES),
+                    op=ALU.add,
+                )
             masked_tiles[b] = masked
 
         def maxima(first, last):
@@ -234,61 +232,60 @@ def tile_contentattention_s_kernel(tc, queries, keys, temperature, bias, out_0, 
                 )
             nc.sync.dma_start(out=out_0[b, n * P : (n + 1) * P, :], in_=attn[:, col, :])
 
-        def denominators(b):
-            for col in range(b * ROW_TILES, (b + 1) * ROW_TILES):
-                nc.vector.scalar_tensor_tensor(
-                    out=denom[:, col : col + 1],
-                    in0=sum_pow[:, col : col + 1],
-                    scalar=exp_part[:, col : col + 1],
-                    in1=ones[:],
-                    op0=ALU.mult,
-                    op1=ALU.add,
-                )
+        def early_denominators(last):
+            nc.vector.tensor_tensor(
+                out=denom[:, 0:last], in0=sum_pow[:, 0:last], in1=exp_part[:, 0:last], op=ALU.mult
+            )
+            nc.vector.tensor_scalar_add(out=denom[:, 0:last], in0=denom[:, 0:last], scalar1=1.0)
+
+        def denominator(col):
+            nc.vector.scalar_tensor_tensor(
+                out=denom[:, col : col + 1],
+                in0=sum_pow[:, col : col + 1],
+                scalar=exp_part[:, col : col + 1],
+                in1=ones[:],
+                op0=ALU.mult,
+                op1=ALU.add,
+            )
 
         vcopy, scopy = nc.vector.tensor_copy, nc.scalar.copy
 
-        def prepare(b, k_copy):
+        def prepare(b, k_copy, q_copy):
             copy_words(k_copy, k_grouped[b], transpose_tiles(k_rows[b], [0, 1]), [0, 1])
-            copy_words(scopy, q_grouped[b], transpose_tiles(q_rows[b], [0, 1]), [0, 1])
+            copy_words(q_copy, q_grouped[b], transpose_tiles(q_rows[b], [0, 1]), [0, 1])
             copy_penalty(scopy, b, transpose_penalty(b))
+            quantize(b)
 
         for n in range(ROW_TILES):
-            copy_words(vcopy, k_grouped[0], transpose_tiles(k_rows[0], [n]), [n])
+            copy_words(scopy, k_grouped[0], transpose_tiles(k_rows[0], [n]), [n])
         for n in range(ROW_TILES):
-            copy_words(scopy, q_grouped[0], transpose_tiles(q_rows[0], [n]), [n])
+            copy_words(vcopy, q_grouped[0], transpose_tiles(q_rows[0], [n]), [n])
         copy_penalty(scopy, 0, transpose_penalty(0))
         quantize(0)
-        prepare(1, vcopy)
-        multiply(0)
+        prepare(1, scopy, vcopy)
         for b in range(B):
-            if b + 2 < B:
-                prepare(b + 2, scopy)
+            multiply(b)
             add_mask(b)
-            if b + 1 < B:
-                quantize(b + 1)
-                multiply(b + 1)
-                maxima(2 * b, 2 * b + 2)
-            else:
-                maxima(2 * b, 2 * b + 1)
-                maxima(2 * b + 1, 2 * b + 2)
+            for col in range(2 * b, 2 * b + 2):
+                maxima(col, col + 1)
+            if b + 2 < B:
+                prepare(b + 2, scopy, scopy)
             exponentials(b)
-            if b + 1 < B:
+            if b < B - 1:
                 powers(2 * b, 2 * b + 2)
-            if 1 <= b < B - 1:
+            if b >= 1:
                 invert(b - 1, b)
                 normalise(b - 1, 0, True)
                 normalise(b - 1, 1, True)
         powers(STATS - 2, STATS - 1)
         powers(STATS - 1, STATS)
         exponential_parts()
-        invert(B - 2, B - 1)
-        normalise(B - 2, 0, False)
-        normalise(B - 2, 1, False)
         invert(B - 1, B)
         normalise(B - 1, 0, True)
-        normalise(B - 1, 1, False)
-        for b in range(B):
-            denominators(b)
+        normalise(B - 1, 1, True)
+        early_denominators(STATS - 2)
+        denominator(STATS - 2)
+        denominator(STATS - 1)
 
         nc.vector.reciprocal(out=conf_cols[:, 0:STATS], in_=denom[:])
         conf_bank = psum.tile([P, BANK], F32, name="bank")

@@ -43,13 +43,14 @@ def tile_contentattention_s_kernel(tc, queries, keys, temperature, bias, out_0, 
         for b in range(B):
             k_sb = per_batch.tile([P, ROW_TILES * D], BF16)
             q_sb = per_batch.tile([P, ROW_TILES * D], BF16)
-            k_tiles = keys[b].rearrange("(n p) d -> p n d", p=P)
-            q_tiles = queries[b].rearrange("(n p) d -> p n d", p=P)
             k_rows.append(k_sb)
             q_rows.append(q_sb)
-            for sb, dram in ((k_sb, k_tiles), (q_sb, q_tiles)):
-                for n in range(ROW_TILES):
-                    nc.sync.dma_start(out=sb[:, n * D : (n + 1) * D], in_=dram[:, n, :])
+            for sb, dram in ((k_sb, keys[b]), (q_sb, queries[b])):
+                if b == 0:
+                    for n in range(ROW_TILES):
+                        nc.sync.dma_start(out=sb[:, n * D : (n + 1) * D], in_=dram[n * P : (n + 1) * P, :])
+                else:
+                    nc.sync.dma_start(out=sb[:], in_=dram.rearrange("(p n) d -> p (n d)", n=ROW_TILES))
 
         ident = consts.tile([P, P], F32)
         nc.vector.memset(ident[:], 0.0)
@@ -117,13 +118,16 @@ def tile_contentattention_s_kernel(tc, queries, keys, temperature, bias, out_0, 
         k_grouped = [group_tile("k_grouped") for b in range(B)]
         q_grouped = [group_tile("q_grouped") for b in range(B)]
 
-        def copy_words(copy, grouped, bank, tiles):
-            first, count = tiles[0], len(tiles)
+        def copy_row_tile(copy, grouped, bank, n):
             copy(
-                out=grouped[:, first * P * PACK : (first + count) * P * PACK]
-                .bitcast(F32)
-                .rearrange("w (n p h) -> w n p h", n=count, h=HALVES),
-                in_=bank[:, 0 : count * HALVES * P].rearrange("w (n h p) -> w n p h", n=count, h=HALVES),
+                out=grouped[:, n * P * PACK : (n + 1) * P * PACK].bitcast(F32).rearrange("w (p h) -> w p h", h=HALVES),
+                in_=bank[:, 0 : HALVES * P].rearrange("w (h p) -> w p h", h=HALVES),
+            )
+
+        def copy_rows(copy, grouped, bank):
+            copy(
+                out=grouped[:].bitcast(F32).rearrange("w (p n h) -> w p n h", n=ROW_TILES, h=HALVES),
+                in_=bank[:].rearrange("w (n h p) -> w p n h", n=ROW_TILES, h=HALVES),
             )
 
         penalties = {}
@@ -166,11 +170,12 @@ def tile_contentattention_s_kernel(tc, queries, keys, temperature, bias, out_0, 
 
         def add_mask(b):
             masked = per_batch.tile([P, ROW_TILES, K], F32)
+            mask = penalties[b][:].rearrange("p (k m) -> p m k" if b == 0 else "p (m k) -> p m k", m=ROW_TILES)
             for n in range(ROW_TILES):
                 nc.vector.tensor_tensor(
                     out=masked[:, n, :].rearrange("p (m k) -> p m k", k=P),
                     in0=logits_banks[b][:, n * K : (n + 1) * K].rearrange("p (m k) -> p m k", k=P),
-                    in1=penalties[b][:].rearrange("p (k m) -> p m k", m=ROW_TILES),
+                    in1=mask,
                     op=ALU.add,
                 )
             masked_tiles[b] = masked
@@ -251,15 +256,15 @@ def tile_contentattention_s_kernel(tc, queries, keys, temperature, bias, out_0, 
         vcopy, scopy = nc.vector.tensor_copy, nc.scalar.copy
 
         def prepare(b, k_copy, q_copy):
-            copy_words(k_copy, k_grouped[b], transpose_tiles(k_rows[b], [0, 1]), [0, 1])
-            copy_words(q_copy, q_grouped[b], transpose_tiles(q_rows[b], [0, 1]), [0, 1])
+            copy_rows(k_copy, k_grouped[b], transpose_tiles(k_rows[b], [0, 1]))
+            copy_rows(q_copy, q_grouped[b], transpose_tiles(q_rows[b], [0, 1]))
             copy_penalty(scopy, b, transpose_penalty(b))
             quantize(b)
 
         for n in range(ROW_TILES):
-            copy_words(scopy, k_grouped[0], transpose_tiles(k_rows[0], [n]), [n])
+            copy_row_tile(scopy, k_grouped[0], transpose_tiles(k_rows[0], [n]), n)
         for n in range(ROW_TILES):
-            copy_words(vcopy, q_grouped[0], transpose_tiles(q_rows[0], [n]), [n])
+            copy_row_tile(vcopy, q_grouped[0], transpose_tiles(q_rows[0], [n]), n)
         copy_penalty(scopy, 0, transpose_penalty(0))
         quantize(0)
         prepare(1, scopy, vcopy)

@@ -33,11 +33,6 @@ def tile_contentattention_s_kernel(tc, queries, keys, temperature, bias, out_0, 
         per_batch = ctx.enter_context(tc.tile_pool(name="per_batch", bufs=B))
         psum = ctx.enter_context(tc.psum_pool(name="psum", bufs=8))
 
-        temp_bf = consts.tile([P, 1], BF16)
-        nc.scalar.dma_start(out=temp_bf[:], in_=temperature.partition_broadcast(P))
-        bias_bf = consts.tile([P, 1], BF16)
-        nc.scalar.dma_start(out=bias_bf[:], in_=bias.partition_broadcast(P))
-
         k_rows = []
         q_rows = []
         for b in range(B):
@@ -52,6 +47,11 @@ def tile_contentattention_s_kernel(tc, queries, keys, temperature, bias, out_0, 
                 else:
                     nc.sync.dma_start(out=sb[:], in_=dram.rearrange("(p n) d -> p (n d)", n=ROW_TILES))
 
+        temp_bf = consts.tile([P, 1], BF16)
+        nc.sync.dma_start(out=temp_bf[:], in_=temperature.partition_broadcast(P))
+        bias_bf = consts.tile([P, 1], BF16)
+        nc.sync.dma_start(out=bias_bf[:], in_=bias.partition_broadcast(P))
+
         ident = consts.tile([P, P], F32)
         nc.vector.memset(ident[:], 0.0)
         make_identity(nc, ident[:], nomemset=True)
@@ -63,14 +63,6 @@ def tile_contentattention_s_kernel(tc, queries, keys, temperature, bias, out_0, 
         nc.vector.memset(scratch[:], 0.0)
         nc.scalar.activation(out=scratch[:], in_=scratch[:], func=ACT.Exp)
 
-        temp = consts.tile([P, 1], F32)
-        nc.vector.tensor_copy(out=temp[:], in_=temp_bf[:])
-        neg_temp = consts.tile([P, 1], F32)
-        nc.vector.tensor_scalar_mul(out=neg_temp[:], in0=temp_bf[:], scalar1=-1.0)
-        neg_bias_temp = consts.tile([P, 1], F32)
-        nc.vector.scalar_tensor_tensor(
-            out=neg_bias_temp[:], in0=bias_bf[:], scalar=-1.0, in1=temp_bf[:], op0=ALU.mult, op1=ALU.mult
-        )
 
         neg_max = consts.tile([P, STATS], F32)
         row_sum = consts.tile([P, STATS], F32)
@@ -91,6 +83,17 @@ def tile_contentattention_s_kernel(tc, queries, keys, temperature, bias, out_0, 
                 op1=ALU.mult,
             )
             penalty_cols.append(penalty_col)
+
+        temp = consts.tile([P, 1], F32)
+        nc.gpsimd.tensor_scalar(
+            out=temp[:], in0=temp_bf[:], scalar1=1.0, scalar2=0.0, op0=ALU.mult, op1=ALU.add
+        )
+        neg_temp = consts.tile([P, 1], F32)
+        nc.gpsimd.tensor_scalar(
+            out=neg_temp[:], in0=temp_bf[:], scalar1=-1.0, scalar2=0.0, op0=ALU.mult, op1=ALU.add
+        )
+        neg_bias_temp = consts.tile([P, 1], F32)
+        nc.gpsimd.tensor_tensor(out=neg_bias_temp[:], in0=bias_bf[:], in1=neg_temp[:], op=ALU.mult)
 
         def words_of(rows, n, h):
             return rows[:].bitcast(F32)[:, n * WORDS + h : (n + 1) * WORDS : HALVES]

@@ -18,6 +18,7 @@ ROW_TILES = Q // P
 PACK = 4
 WORDS = D // 2
 HALVES = WORDS // P
+BLOCK = 32
 BANK = 512
 STATS = B * ROW_TILES
 MASKED = -(2.0**100)
@@ -55,7 +56,7 @@ def tile_contentattention_s_kernel(tc, queries, keys, temperature, bias, out_0, 
         ident = consts.tile([P, P], F32)
         nc.vector.memset(ident[:], 0.0)
         make_identity(nc, ident[:], nomemset=True)
-        conf_cols = consts.tile([P, P], F32)
+        conf_cols = consts.tile([P, BLOCK], F32, align_bytes=64)
         nc.vector.memset(conf_cols[:], 0.0)
         ones = consts.tile([P, 1], F32)
         nc.vector.memset(ones[:], 1.0)
@@ -142,19 +143,18 @@ def tile_contentattention_s_kernel(tc, queries, keys, temperature, bias, out_0, 
 
         codes = {}
 
-        def quantize(b):
-            k_codes = per_batch.tile([P, K], U32, align_bytes=64)
-            k_scales = per_batch.tile([P, K], U8, align_bytes=64)
-            nc.vector.quantize_mx(out=k_codes[:].bitcast(FP8X4), scales=k_scales[:], in_=k_grouped[b][:])
-            q_codes = per_batch.tile([P, Q], U32, align_bytes=64)
-            q_scales = per_batch.tile([P, Q], U8, align_bytes=64)
-            nc.vector.quantize_mx(out=q_codes[:].bitcast(FP8X4), scales=q_scales[:], in_=q_grouped[b][:])
-            codes[b] = (k_codes, k_scales, q_codes, q_scales)
+        def quantize(side, b):
+            operand = per_batch.tile([P, K], U32, align_bytes=64, name="codes_" + side)
+            scales = per_batch.tile([P, K], U8, align_bytes=64, name="scales_" + side)
+            grouped = {"k": k_grouped, "q": q_grouped}[side][b]
+            nc.vector.quantize_mx(out=operand[:].bitcast(FP8X4), scales=scales[:], in_=grouped[:])
+            codes[side, b] = (operand, scales)
 
         logits_banks = {}
 
         def multiply(b):
-            k_codes, k_scales, q_codes, q_scales = codes[b]
+            k_codes, k_scales = codes["k", b]
+            q_codes, q_scales = codes["q", b]
             logits = psum.tile([P, BANK], F32, name="bank")
             for n in range(ROW_TILES):
                 q_cols = slice(n * P, (n + 1) * P)
@@ -258,46 +258,55 @@ def tile_contentattention_s_kernel(tc, queries, keys, temperature, bias, out_0, 
 
         vcopy, scopy = nc.vector.tensor_copy, nc.scalar.copy
 
-        def prepare(b, k_copy, q_copy):
-            copy_rows(k_copy, k_grouped[b], transpose_tiles(k_rows[b], [0, 1]))
-            copy_rows(q_copy, q_grouped[b], transpose_tiles(q_rows[b], [0, 1]))
+        def regroup(b):
+            copy_rows(scopy, k_grouped[b], transpose_tiles(k_rows[b], [0, 1]))
+            copy_rows(scopy, q_grouped[b], transpose_tiles(q_rows[b], [0, 1]))
             copy_penalty(scopy, b, transpose_penalty(b))
-            quantize(b)
 
+        copy_row_tile(scopy, k_grouped[0], transpose_tiles(k_rows[0], [0]), 0)
+        copy_row_tile(vcopy, k_grouped[0], transpose_tiles(k_rows[0], [1]), 1)
         for n in range(ROW_TILES):
-            copy_row_tile(scopy, k_grouped[0], transpose_tiles(k_rows[0], [n]), n)
-        for n in range(ROW_TILES):
-            copy_row_tile(vcopy, q_grouped[0], transpose_tiles(q_rows[0], [n]), n)
+            copy_row_tile(scopy, q_grouped[0], transpose_tiles(q_rows[0], [n]), n)
         copy_penalty(scopy, 0, transpose_penalty(0))
-        quantize(0)
-        prepare(1, scopy, vcopy)
+        quantize("k", 0)
+        quantize("q", 0)
+        regroup(1)
+        quantize("k", 1)
         for b in range(B):
             multiply(b)
             add_mask(b)
+            if b == 0:
+                quantize("q", 1)
             for col in range(2 * b, 2 * b + 2):
                 maxima(col, col + 1)
             if b + 2 < B:
-                prepare(b + 2, scopy, scopy)
+                regroup(b + 2)
+                quantize("k", b + 2)
+                quantize("q", b + 2)
             exponentials(b)
             if b < B - 1:
                 powers(2 * b, 2 * b + 2)
+            else:
+                powers(2 * b, 2 * b + 1)
+                powers(2 * b + 1, 2 * b + 2)
+                exponential_parts()
             if b >= 1:
                 invert(b - 1, b)
                 normalise(b - 1, 0, True)
                 normalise(b - 1, 1, True)
-        powers(STATS - 2, STATS - 1)
-        powers(STATS - 1, STATS)
-        exponential_parts()
+        early_denominators(STATS - 2)
         invert(B - 1, B)
         normalise(B - 1, 0, True)
         normalise(B - 1, 1, True)
-        early_denominators(STATS - 2)
         denominator(STATS - 2)
         denominator(STATS - 1)
 
         nc.vector.reciprocal(out=conf_cols[:, 0:STATS], in_=denom[:])
-        conf_bank = psum.tile([P, BANK], F32, name="bank")
-        nc.tensor.transpose(out=conf_bank[:, 0:P], in_=conf_cols[:], identity=ident[:])
-        conf_rows = consts.tile([STATS, P], F32)
-        nc.vector.tensor_copy(out=conf_rows[:], in_=conf_bank[0:STATS, 0:P])
-        nc.sync.dma_start(out=out_1.rearrange("b (n p) -> (b n) p", p=P), in_=conf_rows[:])
+        conf_rows = consts.tile([P, BLOCK], F32, align_bytes=64)
+        nc.vector.transpose(out=conf_rows[:], in_=conf_cols[:])
+        out_rows = out_1.rearrange("b (n p) -> (b n) p", p=P)
+        for j in range(P // BLOCK):
+            queue = nc.sync if j % 2 == 0 else nc.scalar
+            queue.dma_start(
+                out=out_rows[:, j * BLOCK : (j + 1) * BLOCK], in_=conf_rows[j * BLOCK : j * BLOCK + STATS, :]
+            )

@@ -284,11 +284,9 @@ def tile_contentattention_s_kernel(tc, queries, keys, temperature, bias, out_0, 
                 quantize("k", b + 2)
                 quantize("q", b + 2)
             exponentials(b)
-            if b < B - 1:
-                powers(2 * b, 2 * b + 2)
-            else:
-                powers(2 * b, 2 * b + 1)
-                powers(2 * b + 1, 2 * b + 2)
+            if b >= 1:
+                powers(0 if b == 1 else 2 * b, 2 * b + 2)
+            if b == B - 1:
                 exponential_parts()
             if b >= 1:
                 invert(b - 1, b)

@@ -72,10 +72,11 @@ def tile_contentattention_s_kernel(tc, queries, keys, temperature, bias, out_0, 
         exp_part = consts.tile([P, STATS], F32)
         denom = consts.tile([P, STATS], F32)
 
-        penalty_cols = []
-        for b in range(B):
+        penalty_cols = {}
+
+        def mark_masked(b):
             penalty_col = per_batch.tile([P, ROW_TILES], BF16)
-            nc.gpsimd.tensor_scalar(
+            nc.vector.tensor_scalar(
                 out=penalty_col[:].rearrange("p (n o) -> p n o", o=1),
                 in0=k_rows[b][:].rearrange("p (n d) -> p n d", n=ROW_TILES)[:, :, 0:1],
                 scalar1=0.0,
@@ -83,7 +84,7 @@ def tile_contentattention_s_kernel(tc, queries, keys, temperature, bias, out_0, 
                 op0=ALU.is_equal,
                 op1=ALU.mult,
             )
-            penalty_cols.append(penalty_col)
+            penalty_cols[b] = penalty_col
 
         temp = consts.tile([P, 1], F32)
         nc.gpsimd.tensor_scalar(
@@ -260,27 +261,32 @@ def tile_contentattention_s_kernel(tc, queries, keys, temperature, bias, out_0, 
 
         def regroup(b):
             copy_rows(scopy, k_grouped[b], transpose_tiles(k_rows[b], [0, 1]))
+            copy_penalty(scopy, b - 1, transpose_penalty(b - 1))
             copy_rows(scopy, q_grouped[b], transpose_tiles(q_rows[b], [0, 1]))
-            copy_penalty(scopy, b, transpose_penalty(b))
 
+        mark_masked(0)
         copy_row_tile(scopy, k_grouped[0], transpose_tiles(k_rows[0], [0]), 0)
         copy_row_tile(vcopy, k_grouped[0], transpose_tiles(k_rows[0], [1]), 1)
         for n in range(ROW_TILES):
             copy_row_tile(scopy, q_grouped[0], transpose_tiles(q_rows[0], [n]), n)
-        copy_penalty(scopy, 0, transpose_penalty(0))
         quantize("k", 0)
         quantize("q", 0)
+        mark_masked(1)
         regroup(1)
         quantize("k", 1)
+        mark_masked(2)
         for b in range(B):
             multiply(b)
             add_mask(b)
             if b == 0:
                 quantize("q", 1)
+                mark_masked(3)
             for col in range(2 * b, 2 * b + 2):
                 maxima(col, col + 1)
             if b + 2 < B:
                 regroup(b + 2)
+                if b + 2 == B - 1:
+                    copy_penalty(scopy, B - 1, transpose_penalty(B - 1))
                 quantize("k", b + 2)
                 quantize("q", b + 2)
             exponentials(b)

from contextlib import ExitStack

import concourse.mybir as mybir
from concourse.masks import make_identity

F32 = mybir.dt.float32
BF16 = mybir.dt.bfloat16
U32 = mybir.dt.uint32
U8 = mybir.dt.uint8
FP8X4 = mybir.dt.float8_e4m3fn_x4
ALU = mybir.AluOpType
ACT = mybir.ActivationFunctionType
AXIS = mybir.AxisListType

B, Q, K, D = 4, 256, 256, 512
P = 128
ROW_TILES = Q // P
PACK = 4
WORDS = D // 2
HALVES = WORDS // P
BLOCK = 32
BANK = 512
STATS = B * ROW_TILES
MASKED = -(2.0**100)

FLOPS = 2 * B * Q * K * D


def tile_contentattention_s_kernel(tc, queries, keys, temperature, bias, out_0, out_1):
    nc = tc.nc
    with ExitStack() as ctx:
        ctx.enter_context(tc.manual_schedule())
        consts = ctx.enter_context(tc.tile_pool(name="consts", bufs=1))
        per_batch = ctx.enter_context(tc.tile_pool(name="per_batch", bufs=B))
        psum = ctx.enter_context(tc.psum_pool(name="psum", bufs=8))

        k_rows = []
        q_rows = []
        for b in range(B):
            k_sb = per_batch.tile([P, ROW_TILES * D], BF16)
            q_sb = per_batch.tile([P, ROW_TILES * D], BF16)
            k_rows.append(k_sb)
            q_rows.append(q_sb)
            for sb, dram in ((k_sb, keys[b]), (q_sb, queries[b])):
                if b == 0:
                    for n in range(ROW_TILES):
                        nc.sync.dma_start(out=sb[:, n * D : (n + 1) * D], in_=dram[n * P : (n + 1) * P, :])
                else:
                    nc.sync.dma_start(out=sb[:], in_=dram.rearrange("(p n) d -> p (n d)", n=ROW_TILES))

        temp_bf = consts.tile([P, 1], BF16)
        nc.sync.dma_start(out=temp_bf[:], in_=temperature.partition_broadcast(P))
        bias_bf = consts.tile([P, 1], BF16)
        nc.sync.dma_start(out=bias_bf[:], in_=bias.partition_broadcast(P))

        ident = consts.tile([P, P], F32)
        nc.vector.memset(ident[:], 0.0)
        make_identity(nc, ident[:], nomemset=True)
        conf_cols = consts.tile([P, BLOCK], F32, align_bytes=64)
        nc.vector.memset(conf_cols[:], 0.0)
        ones = consts.tile([P, 1], F32)
        nc.vector.memset(ones[:], 1.0)
        scratch = consts.tile([P, 1], F32)
        nc.vector.memset(scratch[:], 0.0)
        nc.scalar.activation(out=scratch[:], in_=scratch[:], func=ACT.Exp)


        neg_max = consts.tile([P, STATS], F32)
        row_sum = consts.tile([P, STATS], F32)
        inv_sum = consts.tile([P, STATS], F32)
        sum_pow = consts.tile([P, STATS], F32)
        exp_part = consts.tile([P, STATS], F32)
        denom = consts.tile([P, STATS], F32)

        penalty_cols = {}

        def mark_masked(b):
            penalty_col = per_batch.tile([P, ROW_TILES], BF16)
            nc.vector.tensor_scalar(
                out=penalty_col[:].rearrange("p (n o) -> p n o", o=1),
                in0=k_rows[b][:].rearrange("p (n d) -> p n d", n=ROW_TILES)[:, :, 0:1],
                scalar1=0.0,
                scalar2=MASKED,
                op0=ALU.is_equal,
                op1=ALU.mult,
            )
            penalty_cols[b] = penalty_col

        temp = consts.tile([P, 1], F32)
        nc.gpsimd.tensor_scalar(
            out=temp[:], in0=temp_bf[:], scalar1=1.0, scalar2=0.0, op0=ALU.mult, op1=ALU.add
        )
        neg_temp = consts.tile([P, 1], F32)
        nc.gpsimd.tensor_scalar(
            out=neg_temp[:], in0=temp_bf[:], scalar1=-1.0, scalar2=0.0, op0=ALU.mult, op1=ALU.add
        )
        neg_bias_temp = consts.tile([P, 1], F32)
        nc.gpsimd.tensor_tensor(out=neg_bias_temp[:], in0=bias_bf[:], in1=neg_temp[:], op=ALU.mult)

        def words_of(rows, n, h):
            return rows[:].bitcast(F32)[:, n * WORDS + h : (n + 1) * WORDS : HALVES]

        def transpose_tiles(rows, tiles):
            bank = psum.tile([P, BANK], F32, name="bank")
            for i, n in enumerate(tiles):
                for h in range(HALVES):
                    piece = i * HALVES + h
                    nc.tensor.transpose(
                        out=bank[:, piece * P : (piece + 1) * P], in_=words_of(rows, n, h), identity=ident[:]
                    )
            return bank

        def transpose_penalty(b):
            bank = psum.tile([P, BANK], F32, name="bank")
            nc.tensor.transpose(
                out=bank[:, 0:P], in_=penalty_cols[b][:].bitcast(F32).to_broadcast([P, P]), identity=ident[:]
            )
            return bank

        def group_tile(name):
            return per_batch.tile([P, K * PACK], BF16, align_bytes=64, name=name)

        k_grouped = [group_tile("k_grouped") for b in range(B)]
        q_grouped = [group_tile("q_grouped") for b in range(B)]

        def copy_row_tile(copy, grouped, bank, n):
            copy(
                out=grouped[:, n * P * PACK : (n + 1) * P * PACK].bitcast(F32).rearrange("w (p h) -> w p h", h=HALVES),
                in_=bank[:, 0 : HALVES * P].rearrange("w (h p) -> w p h", h=HALVES),
            )

        def copy_rows(copy, grouped, bank):
            copy(
                out=grouped[:].bitcast(F32).rearrange("w (p n h) -> w p n h", n=ROW_TILES, h=HALVES),
                in_=bank[:].rearrange("w (n h p) -> w p n h", n=ROW_TILES, h=HALVES),
            )

        penalties = {}

        def copy_penalty(copy, b, bank):
            penalty = per_batch.tile([P, K], BF16)
            copy(out=penalty[:].bitcast(F32), in_=bank[:, 0:P])
            penalties[b] = penalty

        codes = {}

        def quantize(side, b):
            operand = per_batch.tile([P, K], U32, align_bytes=64, name="codes_" + side)
            scales = per_batch.tile([P, K], U8, align_bytes=64, name="scales_" + side)
            grouped = {"k": k_grouped, "q": q_grouped}[side][b]
            nc.vector.quantize_mx(out=operand[:].bitcast(FP8X4), scales=scales[:], in_=grouped[:])
            codes[side, b] = (operand, scales)

        logits_banks = {}

        def multiply(b):
            k_codes, k_scales = codes["k", b]
            q_codes, q_scales = codes["q", b]
            logits = psum.tile([P, BANK], F32, name="bank")
            for n in range(ROW_TILES):
                q_cols = slice(n * P, (n + 1) * P)
                nc.tensor.matmul_mx(
                    out=logits[:, n * K : (n + 1) * K],
                    lhsT=q_codes[:, q_cols].bitcast(FP8X4),
                    lhsT_scale=q_scales[:, q_cols],
                    rhs=k_codes[:].bitcast(FP8X4),
                    rhs_scale=k_scales[:],
                    start=True,
                    stop=True,
                )
            logits_banks[b] = logits

        masked_tiles = {}

        def add_mask(b):
            masked = per_batch.tile([P, ROW_TILES, K], F32)
            mask = penalties[b][:].rearrange("p (k m) -> p m k" if b == 0 else "p (m k) -> p m k", m=ROW_TILES)
            for n in range(ROW_TILES):
                nc.vector.tensor_tensor(
                    out=masked[:, n, :].rearrange("p (m k) -> p m k", k=P),
                    in0=logits_banks[b][:, n * K : (n + 1) * K].rearrange("p (m k) -> p m k", k=P),
                    in1=mask,
                    op=ALU.add,
                )
            masked_tiles[b] = masked

        def maxima(first, last):
            b, n = divmod(first, ROW_TILES)
            nc.vector.tensor_reduce(
                out=neg_max[:, first:last],
                in_=masked_tiles[b][:, n : n + last - first, :],
                axis=AXIS.X,
                op=ALU.max,
                negate=True,
            )

        exps = {}

        def exponentials(b):
            expd = per_batch.tile([P, ROW_TILES, K], F32)
            for n in range(ROW_TILES):
                col = b * ROW_TILES + n
                nc.scalar.activation(
                    out=expd[:, n, :],
                    in_=masked_tiles[b][:, n, :],
                    func=ACT.Exp,
                    bias=neg_max[:, col : col + 1],
                    accum_out=row_sum[:, col : col + 1],
                )
            exps[b] = expd

        def powers(first, last):
            cols = slice(first, last)
            nc.gpsimd.tensor_tensor(
                out=sum_pow[:, cols],
                in0=row_sum[:, cols],
                in1=neg_temp[:].to_broadcast([P, last - first]),
                op=ALU.pow,
            )

        def exponential_parts():
            nc.scalar.activation(
                out=exp_part[:], in_=neg_max[:], func=ACT.Exp, scale=temp[:], bias=neg_bias_temp[:]
            )

        attn = consts.tile([P, STATS, K], F32)

        def invert(first, last):
            cols = slice(first * ROW_TILES, last * ROW_TILES)
            nc.vector.reciprocal(out=inv_sum[:, cols], in_=row_sum[:, cols])

        def normalise(b, n, on_scalar):
            col = b * ROW_TILES + n
            if on_scalar:
                nc.scalar.activation(
                    out=attn[:, col, :], in_=exps[b][:, n, :], func=ACT.Copy, scale=inv_sum[:, col : col + 1]
                )
            else:
                nc.vector.tensor_scalar_mul(
                    out=attn[:, col, :], in0=exps[b][:, n, :], scalar1=inv_sum[:, col : col + 1]
                )
            nc.sync.dma_start(out=out_0[b, n * P : (n + 1) * P, :], in_=attn[:, col, :])

        def early_denominators(last):
            nc.vector.tensor_tensor(
                out=denom[:, 0:last], in0=sum_pow[:, 0:last], in1=exp_part[:, 0:last], op=ALU.mult
            )
            nc.vector.tensor_scalar_add(out=denom[:, 0:last], in0=denom[:, 0:last], scalar1=1.0)

        def denominator(col):
            nc.vector.scalar_tensor_tensor(
                out=denom[:, col : col + 1],
                in0=sum_pow[:, col : col + 1],
                scalar=exp_part[:, col : col + 1],
                in1=ones[:],
                op0=ALU.mult,
                op1=ALU.add,
            )

        vcopy, scopy = nc.vector.tensor_copy, nc.scalar.copy

        def regroup(b):
            copy_rows(scopy, k_grouped[b], transpose_tiles(k_rows[b], [0, 1]))
            copy_penalty(scopy, b - 1, transpose_penalty(b - 1))
            copy_rows(scopy, q_grouped[b], transpose_tiles(q_rows[b], [0, 1]))

        mark_masked(0)
        copy_row_tile(scopy, k_grouped[0], transpose_tiles(k_rows[0], [0]), 0)
        copy_row_tile(vcopy, k_grouped[0], transpose_tiles(k_rows[0], [1]), 1)
        for n in range(ROW_TILES):
            copy_row_tile(scopy, q_grouped[0], transpose_tiles(q_rows[0], [n]), n)
        quantize("k", 0)
        quantize("q", 0)
        mark_masked(1)
        regroup(1)
        quantize("k", 1)
        mark_masked(2)
        for b in range(B):
            multiply(b)
            add_mask(b)
            if b == 0:
                quantize("q", 1)
                mark_masked(3)
            for col in range(2 * b, 2 * b + 2):
                maxima(col, col + 1)
            if b + 2 < B:
                regroup(b + 2)
                if b + 2 == B - 1:
                    copy_penalty(scopy, B - 1, transpose_penalty(B - 1))
                quantize("k", b + 2)
                quantize("q", b + 2)
            exponentials(b)
            if b >= 1:
                powers(0 if b == 1 else 2 * b, 2 * b + 2)
            if b == B - 1:
                exponential_parts()
            if b >= 1:
                invert(b - 1, b)
                normalise(b - 1, 0, True)
                normalise(b - 1, 1, True)
        early_denominators(STATS - 2)
        invert(B - 1, B)
        normalise(B - 1, 0, True)
        normalise(B - 1, 1, True)
        denominator(STATS - 2)
        denominator(STATS - 1)

        nc.vector.reciprocal(out=conf_cols[:, 0:STATS], in_=denom[:])
        conf_rows = consts.tile([P, BLOCK], F32, align_bytes=64)
        nc.vector.transpose(out=conf_rows[:], in_=conf_cols[:])
        out_rows = out_1.rearrange("b (n p) -> (b n) p", p=P)
        for j in range(P // BLOCK):
            queue = nc.sync if j % 2 == 0 else nc.scalar
            queue.dma_start(
                out=out_rows[:, j * BLOCK : (j + 1) * BLOCK], in_=conf_rows[j * BLOCK : j * BLOCK + STATS, :]
            )
